import numpy as np
import ml_dtypes


def mxq(x, axis, fmt="e4m3"):
    dtype, down = {"e4m3": (ml_dtypes.float8_e4m3fn, 7), "e5m2": (ml_dtypes.float8_e5m2, 14)}[fmt]
    v = np.moveaxis(np.asarray(x, np.float32).astype(ml_dtypes.bfloat16).astype(np.float64), axis, -1)
    blocks = v.reshape(v.shape[:-1] + (-1, 32))
    amax = np.abs(blocks).max(-1, keepdims=True)
    byte = np.maximum(np.where(amax > 0, np.frexp(amax)[1] - 1 + 127, 0) - down, 1)
    scale = np.exp2(byte - 127.0)
    codes = (blocks / scale).astype(np.float32).astype(dtype).astype(np.float64)
    return np.moveaxis((codes * scale).reshape(v.shape), -1, axis)


WIDE = False


def mx_kscale(k):
    if not WIDE:
        return np.ones(k)
    levels = np.array([10, -10, 5, -5, 0])
    a = np.random.permutation(np.resize(levels, k // 512 * 4)).reshape(k // 512, 4)
    idx = np.arange(k)
    return np.exp2(a[idx // 512, idx % 128 // 32])


BF16 = ml_dtypes.bfloat16


def bf(x):
    return np.asarray(x, np.float32).astype(BF16)


def f64(x):
    return np.asarray(x).astype(np.float64)


B, S, D, H = 2, 512, 512, 4
LN_EPS = 1e-5
SIGMA = 1.96


def layer_norm(v, gamma, beta):
    mu = v.mean(-1, keepdims=True)
    var = v.var(-1, keepdims=True)
    return (v - mu) * (1.0 / np.sqrt(var + LN_EPS)) * gamma + beta


def setup_inputs():
    s = mx_kscale(S)
    z = np.random.standard_normal((B, H, S, S)) * SIGMA
    e = np.exp(z - z.max(-1, keepdims=True))
    return {"probs": bf(e / e.sum(-1, keepdims=True) * s),
            "x": bf(np.random.standard_normal((B, S, D)) / s[:, None]),
            "Wv": bf(np.random.standard_normal((H * D, D)) * 0.25 * np.sqrt(S / (H * D))),
            "gamma": bf(1.0 + 0.1 * np.random.standard_normal(D)),
            "beta": bf(0.1 * np.random.standard_normal(D))}


def reference(probs, x, Wv, gamma, beta):
    xf = f64(x)
    ctx = mxq(f64(probs), 3, "e4m3") @ mxq(xf, 1, "e4m3")[:, None]
    merged = ctx.transpose(0, 2, 1, 3).reshape(B, S, H * D)
    y = (mxq(merged, 2, "e4m3") @ mxq(f64(Wv), 0, "e4m3")) + xf
    return layer_norm(y, f64(gamma), f64(beta))

@@ -1,0 +1,288 @@
+from contextlib import ExitStack
+
+import concourse.mybir as mybir
+from concourse.masks import make_identity
+
+FLOPS = 2 * 2 * 4 * 512 * 512 * 512 + 2 * 2 * 512 * 2048 * 512
+
+F32 = mybir.dt.float32
+BF16 = mybir.dt.bfloat16
+U32 = mybir.dt.uint32
+U8 = mybir.dt.uint8
+FP8X4 = mybir.dt.float8_e4m3fn_x4
+ALU = mybir.AluOpType
+ACT = mybir.ActivationFunctionType
+
+P = 128
+PACK = 4
+BATCHES = 2
+HEADS = 4
+TOKENS = 512
+WIDTH = 512
+HALVES = 2
+PAIR = 2
+UNITS_PER_BATCH = TOKENS // P
+UNITS = BATCHES * UNITS_PER_BATCH
+D_TILES = WIDTH // P
+LN_EPS = 1e-5
+
+
+def tile_bertselfattention_pb_kernel(tc, probs, x, Wv, gamma, beta, out):
+    nc = tc.nc
+
+    probs_rows = probs.rearrange("b h (u p e) j -> b u e p h j", u=HALVES, e=PAIR)
+    x_rows = x.rearrange("b (u p e) d -> b p u (e d)", u=HALVES, e=PAIR)
+    out_rows = out.rearrange("b (u p e) d -> b u e p d", u=HALVES, e=PAIR)
+    wv_rows = Wv.rearrange("(h t p) c -> h p t c", t=PACK, p=P)
+
+    with ExitStack() as ctx:
+        const = ctx.enter_context(tc.tile_pool(name="const", bufs=1))
+        resident = ctx.enter_context(tc.tile_pool(name="resident", bufs=1))
+        stage = ctx.enter_context(tc.tile_pool(name="stage", bufs=2))
+        work = ctx.enter_context(tc.tile_pool(name="work", bufs=3))
+        psum_t = ctx.enter_context(tc.psum_pool(name="psum_t", bufs=2))
+        psum_ctx = ctx.enter_context(tc.psum_pool(name="psum_ctx", bufs=4))
+        psum_y = ctx.enter_context(tc.psum_pool(name="psum_y", bufs=2))
+
+        gain_shift_row = const.tile([P, 2 * WIDTH], BF16)
+        nc.vector.memset(gain_shift_row[:], 0.0)
+        nc.scalar.dma_start(out=gain_shift_row[0:1, 0:WIDTH], in_=gamma.unsqueeze(0))
+        nc.scalar.dma_start(out=gain_shift_row[0:1, WIDTH : 2 * WIDTH], in_=beta.unsqueeze(0))
+
+        probs_raw = [
+            resident.tile([P, HEADS * TOKENS], BF16, name="probs_raw%d" % n) for n in range(UNITS)
+        ]
+        x_raw = [resident.tile([P, PACK * WIDTH], BF16, name="x_raw%d" % b) for b in range(BATCHES)]
+        wv_raw = [resident.tile([P, PACK * WIDTH], BF16, name="wv_raw%d" % h) for h in range(HEADS)]
+
+        def load_probs(n):
+            b, r = divmod(n, UNITS_PER_BATCH)
+            u, e = divmod(r, PAIR)
+            nc.sync.dma_start(
+                out=probs_raw[n][:].rearrange("p (h j) -> p h j", h=HEADS), in_=probs_rows[b, u, e]
+            )
+
+        def load_x(b):
+            nc.sync.dma_start(out=x_raw[b][:].rearrange("p (u f) -> p u f", u=HALVES), in_=x_rows[b])
+
+        def load_wv(h):
+            nc.sync.dma_start(out=wv_raw[h][:].rearrange("p (t c) -> p t c", t=PACK), in_=wv_rows[h])
+
+        load_probs(0)
+        load_x(0)
+        load_probs(1)
+        load_wv(0)
+        load_wv(1)
+        load_probs(2)
+        load_wv(2)
+        load_wv(3)
+        load_probs(3)
+        load_x(1)
+        for n in range(UNITS_PER_BATCH, UNITS):
+            load_probs(n)
+
+        identity = const.tile([P, P], F32)
+        make_identity(nc, identity[:])
+        ones = const.tile([P, P], BF16)
+        nc.vector.memset(ones[:], 1.0)
+        eps = const.tile([P, 1], F32)
+        nc.vector.memset(eps[:], LN_EPS)
+        table_warm = const.tile([P, 1], F32)
+        nc.scalar.activation(out=table_warm[:], in_=eps[:], func=ACT.Sqrt)
+
+        gain = const.tile([P, WIDTH], F32)
+        shift = const.tile([P, WIDTH], F32)
+        for spread, first_column in ((gain, 0), (shift, WIDTH)):
+            spread_ps = psum_y.tile([P, WIDTH], F32, tag="y_ps")
+            nc.tensor.matmul(
+                out=spread_ps[:],
+                lhsT=ones[:],
+                rhs=gain_shift_row[:, first_column : first_column + WIDTH],
+                start=True,
+                stop=True,
+            )
+            nc.scalar.copy(out=spread[:], in_=spread_ps[:])
+
+        x_codes = [resident.tile([P, WIDTH], U32, name="x_codes%d" % b, align_bytes=64) for b in range(BATCHES)]
+        x_scales = [resident.tile([P, WIDTH], U8, name="x_scales%d" % b, align_bytes=64) for b in range(BATCHES)]
+        wv_codes = [resident.tile([P, WIDTH], U32, name="wv_codes%d" % h, align_bytes=64) for h in range(HEADS)]
+        wv_scales = [resident.tile([P, WIDTH], U8, name="wv_scales%d" % h, align_bytes=64) for h in range(HEADS)]
+
+        def regroup_rows(raw):
+            grouped = stage.tile([P, WIDTH * PACK], BF16, tag="rows_grouped", bufs=4, align_bytes=64)
+            nc.vector.tensor_copy(
+                out=grouped[:].rearrange("p (c i t) -> p c t i", i=4, t=PACK),
+                in_=raw[:].rearrange("p (t c i) -> p c t i", t=PACK, i=4),
+            )
+            return grouped
+
+        def quantise(grouped, codes, scales):
+            nc.vector.quantize_mx(out=codes[:].bitcast(FP8X4), scales=scales[:], in_=grouped[:])
+
+        def prepare_values(b):
+            quantise(regroup_rows(x_raw[b]), x_codes[b], x_scales[b])
+
+        def prepare_weights(first_head):
+            grouped = [regroup_rows(wv_raw[h]) for h in (first_head, first_head + 1)]
+            for which in range(2):
+                quantise(grouped[which], wv_codes[first_head + which], wv_scales[first_head + which])
+
+        live = {}
+
+        def transpose_probs(n):
+            words = probs_raw[n][:].bitcast(F32)
+            for head_pair in range(HEADS // 2):
+                flipped = psum_t.tile([P, 2, HALVES, P], F32, tag="flipped")
+                for hh in range(2):
+                    for u in range(HALVES):
+                        first = ((2 * head_pair + hh) * HALVES + u) * P
+                        nc.tensor.transpose(flipped[:, hh, u, :], words[:, first : first + P], identity[:])
+                live["flipped%d" % head_pair, n] = flipped
+
+        def regroup_probs(n):
+            grouped = stage.tile([P, HEADS * P * PACK], BF16, tag="probs_grouped", align_bytes=64)
+            grouped_words = grouped[:].bitcast(F32).rearrange("p (h i u) -> p h i u", h=HEADS, u=HALVES)
+            for head_pair in range(HEADS // 2):
+                nc.scalar.copy(
+                    out=grouped_words[:, 2 * head_pair : 2 * head_pair + 2],
+                    in_=live["flipped%d" % head_pair, n][:].rearrange("p h u i -> p h i u"),
+                )
+            live["probs_grouped", n] = grouped
+
+        def quantise_probs(n):
+            codes = stage.tile([P, HEADS * P], U32, tag="probs_codes", align_bytes=64)
+            scales = stage.tile([P, HEADS * P], U8, tag="probs_scales", align_bytes=64)
+            quantise(live["probs_grouped", n], codes, scales)
+            live["probs_codes", n] = codes
+            live["probs_scales", n] = scales
+
+        def pool_values(n):
+            b = n // UNITS_PER_BATCH
+            for h in range(HEADS):
+                tokens = slice(h * P, (h + 1) * P)
+                ctx_ps = psum_ctx.tile([P, D_TILES, P], F32, tag="ctx_ps")
+                for t in range(D_TILES):
+                    d_columns = slice(t * P, (t + 1) * P)
+                    nc.tensor.matmul_mx(
+                        out=ctx_ps[:, t, :],
+                        lhsT=x_codes[b][:, d_columns].bitcast(FP8X4),
+                        lhsT_scale=x_scales[b][:, d_columns],
+                        rhs=live["probs_codes", n][:, tokens].bitcast(FP8X4),
+                        rhs_scale=live["probs_scales", n][:, tokens],
+                        start=True,
+                        stop=True,
+                    )
+                live["ctx_ps%d" % h, n] = ctx_ps
+
+        def regroup_ctx(n):
+            grouped = stage.tile([P, HEADS * P * PACK], BF16, tag="ctx_grouped", align_bytes=64)
+            by_head = grouped[:].rearrange("p (h i t) -> p h i t", h=HEADS, t=PACK)
+            for h in range(HEADS):
+                nc.scalar.copy(out=by_head[:, h], in_=live["ctx_ps%d" % h, n][:].rearrange("p t i -> p i t"))
+            live["ctx_grouped", n] = grouped
+
+        def quantise_ctx(n):
+            codes = stage.tile([P, HEADS * P], U32, tag="ctx_codes", align_bytes=64)
+            scales = stage.tile([P, HEADS * P], U8, tag="ctx_scales", align_bytes=64)
+            quantise(live["ctx_grouped", n], codes, scales)
+            live["ctx_codes", n] = codes
+            live["ctx_scales", n] = scales
+
+        def merge_heads(n):
+            y_ps = psum_y.tile([P, WIDTH], F32, tag="y_ps")
+            for h in range(HEADS):
+                tokens = slice(h * P, (h + 1) * P)
+                nc.tensor.matmul_mx(
+                    out=y_ps[:],
+                    lhsT=live["ctx_codes", n][:, tokens].bitcast(FP8X4),
+                    lhsT_scale=live["ctx_scales", n][:, tokens],
+                    rhs=wv_codes[h][:].bitcast(FP8X4),
+                    rhs_scale=wv_scales[h][:],
+                    start=(h == 0),
+                    stop=(h == HEADS - 1),
+                )
+            live["y_ps", n] = y_ps
+
+        def add_residual(n):
+            b, r = divmod(n, UNITS_PER_BATCH)
+            y = work.tile([P, WIDTH], F32, tag="y")
+            y_sum = work.tile([P, 1], F32, tag="y_sum")
+            nc.vector.scalar_tensor_tensor(
+                out=y[:],
+                in0=live["y_ps", n][:],
+                scalar=1.0,
+                in1=x_raw[b][:, r * WIDTH : (r + 1) * WIDTH],
+                op0=ALU.mult,
+                op1=ALU.add,
+                accum_out=y_sum[:],
+            )
+            minus_mean = work.tile([P, 1], F32, tag="minus_mean")
+            nc.vector.tensor_scalar_mul(minus_mean[:], y_sum[:], -1.0 / WIDTH)
+            live["y", n] = y
+            live["minus_mean", n] = minus_mean
+
+        def centre_and_gain(n):
+            centred = work.tile([P, WIDTH], F32, tag="centred")
+            nc.vector.scalar_tensor_tensor(
+                out=centred[:],
+                in0=live["y", n][:],
+                scalar=live["minus_mean", n][:],
+                in1=gain[:],
+                op0=ALU.add,
+                op1=ALU.mult,
+            )
+            live["centred", n] = centred
+
+        def deviation(n):
+            squares = work.tile([P, WIDTH], BF16, tag="squares")
+            square_sum = work.tile([P, 1], F32, tag="square_sum")
+            nc.scalar.activation(
+                out=squares[:],
+                in_=live["y", n][:],
+                func=ACT.Square,
+                bias=live["minus_mean", n][:],
+                scale=1.0,
+                accum_out=square_sum[:],
+            )
+            std = work.tile([P, 1], F32, tag="std")
+            nc.scalar.activation(out=std[:], in_=square_sum[:], func=ACT.Sqrt, bias=eps[:], scale=1.0 / WIDTH)
+            live["std", n] = std
+
+        def scale_shift_store(n):
+            b, r = divmod(n, UNITS_PER_BATCH)
+            u, e = divmod(r, PAIR)
+            inv_std = work.tile([P, 1], F32, tag="inv_std")
+            nc.vector.reciprocal(inv_std[:], live["std", n][:])
+            result = work.tile([P, WIDTH], F32, tag="result")
+            nc.vector.scalar_tensor_tensor(
+                out=result[:],
+                in0=live["centred", n][:],
+                scalar=inv_std[:],
+                in1=shift[:],
+                op0=ALU.mult,
+                op1=ALU.add,
+            )
+            nc.sync.dma_start(out=out_rows[b, u, e], in_=result[:])
+
+        def run(step, n):
+            if 0 <= n < UNITS:
+                step(n)
+
+        for k in range(-2, UNITS + 2):
+            run(merge_heads, k - 1)
+            run(scale_shift_store, k - 2)
+            run(add_residual, k - 1)
+            run(regroup_probs, k + 1)
+            run(transpose_probs, k + 2)
+            if k == -2:
+                prepare_values(0)
+            run(quantise_probs, k + 1)
+            if k == -1 or k == 0:
+                prepare_weights(2 * (k + 1))
+            if k == UNITS_PER_BATCH - 3:
+                prepare_values(1)
+            run(centre_and_gain, k - 1)
+            run(regroup_ctx, k)
+            run(pool_values, k + 1)
+            run(quantise_ctx, k)
+            run(deviation, k - 1)

@@ -23,8 +23,12 @@ HALVES = 2
 PAIR = 2
 UNITS_PER_BATCH = TOKENS // P
 UNITS = BATCHES * UNITS_PER_BATCH
-D_TILES = WIDTH // P
+D_PIECES = WIDTH // P
+HEADS_PER_BANK = 2
+RUN = 4
 LN_EPS = 1e-5
+FIRST_ROUND = -2
+LAG = 2
 
 
 def tile_bertselfattention_pb_kernel(tc, probs, x, Wv, gamma, beta, out):
@@ -35,51 +39,71 @@ def tile_bertselfattention_pb_kernel(tc, probs, x, Wv, gamma, beta, out):
     out_rows = out.rearrange("b (u p e) d -> b u e p d", u=HALVES, e=PAIR)
     wv_rows = Wv.rearrange("(h t p) c -> h p t c", t=PACK, p=P)
 
-    with ExitStack() as ctx:
-        const = ctx.enter_context(tc.tile_pool(name="const", bufs=1))
-        resident = ctx.enter_context(tc.tile_pool(name="resident", bufs=1))
-        stage = ctx.enter_context(tc.tile_pool(name="stage", bufs=2))
-        work = ctx.enter_context(tc.tile_pool(name="work", bufs=3))
-        psum_t = ctx.enter_context(tc.psum_pool(name="psum_t", bufs=2))
-        psum_ctx = ctx.enter_context(tc.psum_pool(name="psum_ctx", bufs=4))
-        psum_y = ctx.enter_context(tc.psum_pool(name="psum_y", bufs=2))
+    with ExitStack() as stack:
+        const = stack.enter_context(tc.tile_pool(name="const", bufs=1))
+        resident = stack.enter_context(tc.tile_pool(name="resident", bufs=1))
+        stage = stack.enter_context(tc.tile_pool(name="stage", bufs=3))
+        work = stack.enter_context(tc.tile_pool(name="work", bufs=LAG + 2))
+        psum_t = stack.enter_context(tc.psum_pool(name="psum_t", bufs=HEADS // HEADS_PER_BANK))
+        psum_ctx = stack.enter_context(tc.psum_pool(name="psum_ctx", bufs=HEADS))
+        psum_y = stack.enter_context(tc.psum_pool(name="psum_y", bufs=2))
+        stack.enter_context(tc.manual_schedule())
+
+        def leading_operand(label, source):
+            return {
+                "source": source,
+                "raw": resident.tile([P, PACK * WIDTH], BF16, name="raw_" + label),
+                "codes": resident.tile([P, WIDTH], U32, name="codes_" + label, align_bytes=64),
+                "scales": resident.tile([P, WIDTH], U8, name="scales_" + label, align_bytes=64),
+            }
+
+        x_operands = [leading_operand("x%d" % b, x_rows[b]) for b in range(BATCHES)]
+        wv_operands = [leading_operand("wv%d" % h, wv_rows[h]) for h in range(HEADS)]
+        in_order_of_need = [x_operands[0]] + wv_operands + [x_operands[1]]
+
+        def operands_of_round(k):
+            if k == FIRST_ROUND:
+                return in_order_of_need[0:2]
+            following = k - FIRST_ROUND + 1
+            return in_order_of_need[following : following + 1]
+
+        def load_operand(operand):
+            runs = operand["source"].shape[1]
+            nc.sync.dma_start(
+                out=operand["raw"][:].rearrange("p (r f) -> p r f", r=runs), in_=operand["source"]
+            )
+
+        def regroup_operand(operand):
+            grouped = stage.tile([P, WIDTH * PACK], BF16, tag="operand_grouped", align_bytes=64)
+            nc.vector.tensor_copy(
+                out=grouped[:].rearrange("p (c i t) -> p c t i", i=RUN, t=PACK),
+                in_=operand["raw"][:].rearrange("p (t c i) -> p c t i", t=PACK, i=RUN),
+            )
+            operand["grouped"] = grouped
+
+        def quantise(grouped, codes, scales):
+            nc.vector.quantize_mx(out=codes[:].bitcast(FP8X4), scales=scales[:], in_=grouped[:])
+
+        def quantise_operand(operand):
+            quantise(operand["grouped"], operand["codes"], operand["scales"])
 
         gain_shift_row = const.tile([P, 2 * WIDTH], BF16)
         nc.vector.memset(gain_shift_row[:], 0.0)
-        nc.scalar.dma_start(out=gain_shift_row[0:1, 0:WIDTH], in_=gamma.unsqueeze(0))
-        nc.scalar.dma_start(out=gain_shift_row[0:1, WIDTH : 2 * WIDTH], in_=beta.unsqueeze(0))
 
         probs_raw = [
             resident.tile([P, HEADS * TOKENS], BF16, name="probs_raw%d" % n) for n in range(UNITS)
         ]
-        x_raw = [resident.tile([P, PACK * WIDTH], BF16, name="x_raw%d" % b) for b in range(BATCHES)]
-        wv_raw = [resident.tile([P, PACK * WIDTH], BF16, name="wv_raw%d" % h) for h in range(HEADS)]
-
-        def load_probs(n):
-            b, r = divmod(n, UNITS_PER_BATCH)
-            u, e = divmod(r, PAIR)
+        for n in range(UNITS):
+            b, place = divmod(n, UNITS_PER_BATCH)
+            u, e = divmod(place, PAIR)
             nc.sync.dma_start(
                 out=probs_raw[n][:].rearrange("p (h j) -> p h j", h=HEADS), in_=probs_rows[b, u, e]
             )
-
-        def load_x(b):
-            nc.sync.dma_start(out=x_raw[b][:].rearrange("p (u f) -> p u f", u=HALVES), in_=x_rows[b])
-
-        def load_wv(h):
-            nc.sync.dma_start(out=wv_raw[h][:].rearrange("p (t c) -> p t c", t=PACK), in_=wv_rows[h])
-
-        load_probs(0)
-        load_x(0)
-        load_probs(1)
-        load_wv(0)
-        load_wv(1)
-        load_probs(2)
-        load_wv(2)
-        load_wv(3)
-        load_probs(3)
-        load_x(1)
-        for n in range(UNITS_PER_BATCH, UNITS):
-            load_probs(n)
+            for operand in operands_of_round(n + FIRST_ROUND):
+                load_operand(operand)
+            if n == 0:
+                nc.sync.dma_start(out=gain_shift_row[0:1, 0:WIDTH], in_=gamma.unsqueeze(0))
+                nc.sync.dma_start(out=gain_shift_row[0:1, WIDTH : 2 * WIDTH], in_=beta.unsqueeze(0))
 
         identity = const.tile([P, P], F32)
         make_identity(nc, identity[:])
@@ -88,64 +112,42 @@ def tile_bertselfattention_pb_kernel(tc, probs, x, Wv, gamma, beta, out):
         eps = const.tile([P, 1], F32)
         nc.vector.memset(eps[:], LN_EPS)
         table_warm = const.tile([P, 1], F32)
-        nc.scalar.activation(out=table_warm[:], in_=eps[:], func=ACT.Sqrt)
+        nc.scalar.activation(out=table_warm[:], in_=eps[:], func=ACT.Abs_reciprocal_sqrt)
 
         gain = const.tile([P, WIDTH], F32)
         shift = const.tile([P, WIDTH], F32)
-        for spread, first_column in ((gain, 0), (shift, WIDTH)):
-            spread_ps = psum_y.tile([P, WIDTH], F32, tag="y_ps")
-            nc.tensor.matmul(
-                out=spread_ps[:],
-                lhsT=ones[:],
-                rhs=gain_shift_row[:, first_column : first_column + WIDTH],
-                start=True,
-                stop=True,
-            )
-            nc.scalar.copy(out=spread[:], in_=spread_ps[:])
 
-        x_codes = [resident.tile([P, WIDTH], U32, name="x_codes%d" % b, align_bytes=64) for b in range(BATCHES)]
-        x_scales = [resident.tile([P, WIDTH], U8, name="x_scales%d" % b, align_bytes=64) for b in range(BATCHES)]
-        wv_codes = [resident.tile([P, WIDTH], U32, name="wv_codes%d" % h, align_bytes=64) for h in range(HEADS)]
-        wv_scales = [resident.tile([P, WIDTH], U8, name="wv_scales%d" % h, align_bytes=64) for h in range(HEADS)]
-
-        def regroup_rows(raw):
-            grouped = stage.tile([P, WIDTH * PACK], BF16, tag="rows_grouped", bufs=4, align_bytes=64)
-            nc.vector.tensor_copy(
-                out=grouped[:].rearrange("p (c i t) -> p c t i", i=4, t=PACK),
-                in_=raw[:].rearrange("p (t c i) -> p c t i", t=PACK, i=4),
-            )
-            return grouped
-
-        def quantise(grouped, codes, scales):
-            nc.vector.quantize_mx(out=codes[:].bitcast(FP8X4), scales=scales[:], in_=grouped[:])
-
-        def prepare_values(b):
-            quantise(regroup_rows(x_raw[b]), x_codes[b], x_scales[b])
-
-        def prepare_weights(first_head):
-            grouped = [regroup_rows(wv_raw[h]) for h in (first_head, first_head + 1)]
-            for which in range(2):
-                quantise(grouped[which], wv_codes[first_head + which], wv_scales[first_head + which])
+        def spread_gain_and_shift():
+            for spread, first_column in ((gain, 0), (shift, WIDTH)):
+                spread_ps = psum_y.tile([P, WIDTH], F32, tag="y_ps")
+                nc.tensor.matmul(
+                    out=spread_ps[:],
+                    lhsT=ones[:],
+                    rhs=gain_shift_row[:, first_column : first_column + WIDTH],
+                    start=True,
+                    stop=True,
+                )
+                nc.scalar.copy(out=spread[:], in_=spread_ps[:])
 
         live = {}
 
         def transpose_probs(n):
             words = probs_raw[n][:].bitcast(F32)
-            for head_pair in range(HEADS // 2):
-                flipped = psum_t.tile([P, 2, HALVES, P], F32, tag="flipped")
-                for hh in range(2):
+            for bank in range(HEADS // HEADS_PER_BANK):
+                flipped = psum_t.tile([P, HEADS_PER_BANK, HALVES, P], F32, tag="flipped")
+                for hh in range(HEADS_PER_BANK):
                     for u in range(HALVES):
-                        first = ((2 * head_pair + hh) * HALVES + u) * P
+                        first = ((bank * HEADS_PER_BANK + hh) * HALVES + u) * P
                         nc.tensor.transpose(flipped[:, hh, u, :], words[:, first : first + P], identity[:])
-                live["flipped%d" % head_pair, n] = flipped
+                live["flipped%d" % bank, n] = flipped
 
         def regroup_probs(n):
             grouped = stage.tile([P, HEADS * P * PACK], BF16, tag="probs_grouped", align_bytes=64)
             grouped_words = grouped[:].bitcast(F32).rearrange("p (h i u) -> p h i u", h=HEADS, u=HALVES)
-            for head_pair in range(HEADS // 2):
+            for bank in range(HEADS // HEADS_PER_BANK):
                 nc.scalar.copy(
-                    out=grouped_words[:, 2 * head_pair : 2 * head_pair + 2],
-                    in_=live["flipped%d" % head_pair, n][:].rearrange("p h u i -> p h i u"),
+                    out=grouped_words[:, bank * HEADS_PER_BANK : (bank + 1) * HEADS_PER_BANK],
+                    in_=live["flipped%d" % bank, n][:].rearrange("p h u i -> p h i u"),
                 )
             live["probs_grouped", n] = grouped
 
@@ -156,17 +158,17 @@ def tile_bertselfattention_pb_kernel(tc, probs, x, Wv, gamma, beta, out):
             live["probs_codes", n] = codes
             live["probs_scales", n] = scales
 
-        def pool_values(n):
-            b = n // UNITS_PER_BATCH
+        def first_product(n):
+            x_operand = x_operands[n // UNITS_PER_BATCH]
             for h in range(HEADS):
                 tokens = slice(h * P, (h + 1) * P)
-                ctx_ps = psum_ctx.tile([P, D_TILES, P], F32, tag="ctx_ps")
-                for t in range(D_TILES):
+                ctx_ps = psum_ctx.tile([P, D_PIECES, P], F32, tag="ctx_ps")
+                for t in range(D_PIECES):
                     d_columns = slice(t * P, (t + 1) * P)
                     nc.tensor.matmul_mx(
                         out=ctx_ps[:, t, :],
-                        lhsT=x_codes[b][:, d_columns].bitcast(FP8X4),
-                        lhsT_scale=x_scales[b][:, d_columns],
+                        lhsT=x_operand["codes"][:, d_columns].bitcast(FP8X4),
+                        lhsT_scale=x_operand["scales"][:, d_columns],
                         rhs=live["probs_codes", n][:, tokens].bitcast(FP8X4),
                         rhs_scale=live["probs_scales", n][:, tokens],
                         start=True,
@@ -182,13 +184,13 @@ def tile_bertselfattention_pb_kernel(tc, probs, x, Wv, gamma, beta, out):
             live["ctx_grouped", n] = grouped
 
         def quantise_ctx(n):
-            codes = stage.tile([P, HEADS * P], U32, tag="ctx_codes", align_bytes=64)
-            scales = stage.tile([P, HEADS * P], U8, tag="ctx_scales", align_bytes=64)
+            codes = work.tile([P, HEADS * P], U32, tag="ctx_codes", align_bytes=64)
+            scales = work.tile([P, HEADS * P], U8, tag="ctx_scales", align_bytes=64)
             quantise(live["ctx_grouped", n], codes, scales)
             live["ctx_codes", n] = codes
             live["ctx_scales", n] = scales
 
-        def merge_heads(n):
+        def second_product(n):
             y_ps = psum_y.tile([P, WIDTH], F32, tag="y_ps")
             for h in range(HEADS):
                 tokens = slice(h * P, (h + 1) * P)
@@ -196,22 +198,22 @@ def tile_bertselfattention_pb_kernel(tc, probs, x, Wv, gamma, beta, out):
                     out=y_ps[:],
                     lhsT=live["ctx_codes", n][:, tokens].bitcast(FP8X4),
                     lhsT_scale=live["ctx_scales", n][:, tokens],
-                    rhs=wv_codes[h][:].bitcast(FP8X4),
-                    rhs_scale=wv_scales[h][:],
+                    rhs=wv_operands[h]["codes"][:].bitcast(FP8X4),
+                    rhs_scale=wv_operands[h]["scales"][:],
                     start=(h == 0),
                     stop=(h == HEADS - 1),
                 )
             live["y_ps", n] = y_ps
 
         def add_residual(n):
-            b, r = divmod(n, UNITS_PER_BATCH)
+            b, place = divmod(n, UNITS_PER_BATCH)
             y = work.tile([P, WIDTH], F32, tag="y")
             y_sum = work.tile([P, 1], F32, tag="y_sum")
             nc.vector.scalar_tensor_tensor(
                 out=y[:],
                 in0=live["y_ps", n][:],
                 scalar=1.0,
-                in1=x_raw[b][:, r * WIDTH : (r + 1) * WIDTH],
+                in1=x_operands[b]["raw"][:, place * WIDTH : (place + 1) * WIDTH],
                 op0=ALU.mult,
                 op1=ALU.add,
                 accum_out=y_sum[:],
@@ -233,7 +235,7 @@ def tile_bertselfattention_pb_kernel(tc, probs, x, Wv, gamma, beta, out):
             )
             live["centred", n] = centred
 
-        def deviation(n):
+        def inverse_deviation(n):
             squares = work.tile([P, WIDTH], BF16, tag="squares")
             square_sum = work.tile([P, 1], F32, tag="square_sum")
             nc.scalar.activation(
@@ -244,20 +246,20 @@ def tile_bertselfattention_pb_kernel(tc, probs, x, Wv, gamma, beta, out):
                 scale=1.0,
                 accum_out=square_sum[:],
             )
-            std = work.tile([P, 1], F32, tag="std")
-            nc.scalar.activation(out=std[:], in_=square_sum[:], func=ACT.Sqrt, bias=eps[:], scale=1.0 / WIDTH)
-            live["std", n] = std
+            inv_std = work.tile([P, 1], F32, tag="inv_std")
+            nc.scalar.activation(
+                out=inv_std[:], in_=square_sum[:], func=ACT.Abs_reciprocal_sqrt, bias=eps[:], scale=1.0 / WIDTH
+            )
+            live["inv_std", n] = inv_std
 
         def scale_shift_store(n):
-            b, r = divmod(n, UNITS_PER_BATCH)
-            u, e = divmod(r, PAIR)
-            inv_std = work.tile([P, 1], F32, tag="inv_std")
-            nc.vector.reciprocal(inv_std[:], live["std", n][:])
+            b, place = divmod(n, UNITS_PER_BATCH)
+            u, e = divmod(place, PAIR)
             result = work.tile([P, WIDTH], F32, tag="result")
             nc.vector.scalar_tensor_tensor(
                 out=result[:],
                 in0=live["centred", n][:],
-                scalar=inv_std[:],
+                scalar=live["inv_std", n][:],
                 in1=shift[:],
                 op0=ALU.mult,
                 op1=ALU.add,
@@ -268,21 +270,22 @@ def tile_bertselfattention_pb_kernel(tc, probs, x, Wv, gamma, beta, out):
             if 0 <= n < UNITS:
                 step(n)
 
-        for k in range(-2, UNITS + 2):
-            run(merge_heads, k - 1)
-            run(scale_shift_store, k - 2)
-            run(add_residual, k - 1)
+        for k in range(FIRST_ROUND, UNITS + LAG + 1):
+            operands = operands_of_round(k)
+            run(second_product, k - LAG)
             run(regroup_probs, k + 1)
+            if k == FIRST_ROUND + 1:
+                spread_gain_and_shift()
             run(transpose_probs, k + 2)
-            if k == -2:
-                prepare_values(0)
             run(quantise_probs, k + 1)
-            if k == -1 or k == 0:
-                prepare_weights(2 * (k + 1))
-            if k == UNITS_PER_BATCH - 3:
-                prepare_values(1)
-            run(centre_and_gain, k - 1)
+            run(add_residual, k - LAG)
+            for operand in operands:
+                regroup_operand(operand)
+            run(scale_shift_store, k - LAG - 1)
             run(regroup_ctx, k)
-            run(pool_values, k + 1)
+            run(first_product, k + 1)
+            run(inverse_deviation, k - LAG)
+            run(centre_and_gain, k - LAG)
             run(quantise_ctx, k)
-            run(deviation, k - 1)
+            for operand in operands:
+                quantise_operand(operand)

@@ -47,7 +47,6 @@ def tile_bertselfattention_pb_kernel(tc, probs, x, Wv, gamma, beta, out):
         psum_t = stack.enter_context(tc.psum_pool(name="psum_t", bufs=HEADS // HEADS_PER_BANK))
         psum_ctx = stack.enter_context(tc.psum_pool(name="psum_ctx", bufs=HEADS))
         psum_y = stack.enter_context(tc.psum_pool(name="psum_y", bufs=2))
-        stack.enter_context(tc.manual_schedule())
 
         def leading_operand(label, source):
             return {

@@ -28,7 +28,9 @@ HEADS_PER_BANK = 2
 RUN = 4
 LN_EPS = 1e-5
 FIRST_ROUND = -2
-LAG = 2
+LAG_ADD = 2
+LAG_DEVIATION = 3
+LAG_STORE = 4
 
 
 def tile_bertselfattention_pb_kernel(tc, probs, x, Wv, gamma, beta, out):
@@ -43,10 +45,11 @@ def tile_bertselfattention_pb_kernel(tc, probs, x, Wv, gamma, beta, out):
         const = stack.enter_context(tc.tile_pool(name="const", bufs=1))
         resident = stack.enter_context(tc.tile_pool(name="resident", bufs=1))
         stage = stack.enter_context(tc.tile_pool(name="stage", bufs=3))
-        work = stack.enter_context(tc.tile_pool(name="work", bufs=LAG + 2))
+        work = stack.enter_context(tc.tile_pool(name="work", bufs=LAG_STORE + 1))
         psum_t = stack.enter_context(tc.psum_pool(name="psum_t", bufs=HEADS // HEADS_PER_BANK))
         psum_ctx = stack.enter_context(tc.psum_pool(name="psum_ctx", bufs=HEADS))
         psum_y = stack.enter_context(tc.psum_pool(name="psum_y", bufs=2))
+        stack.enter_context(tc.manual_schedule())
 
         def leading_operand(label, source):
             return {
@@ -62,7 +65,9 @@ def tile_bertselfattention_pb_kernel(tc, probs, x, Wv, gamma, beta, out):
 
         def operands_of_round(k):
             if k == FIRST_ROUND:
-                return in_order_of_need[0:2]
+                return in_order_of_need[0:1]
+            if k == FIRST_ROUND + 1:
+                return in_order_of_need[1:3]
             following = k - FIRST_ROUND + 1
             return in_order_of_need[following : following + 1]
 
@@ -269,22 +274,22 @@ def tile_bertselfattention_pb_kernel(tc, probs, x, Wv, gamma, beta, out):
             if 0 <= n < UNITS:
                 step(n)
 
-        for k in range(FIRST_ROUND, UNITS + LAG + 1):
+        for k in range(FIRST_ROUND, UNITS + LAG_STORE):
             operands = operands_of_round(k)
-            run(second_product, k - LAG)
+            run(second_product, k - LAG_ADD)
             run(regroup_probs, k + 1)
             if k == FIRST_ROUND + 1:
                 spread_gain_and_shift()
             run(transpose_probs, k + 2)
             run(quantise_probs, k + 1)
-            run(add_residual, k - LAG)
+            run(add_residual, k - LAG_ADD)
             for operand in operands:
                 regroup_operand(operand)
-            run(scale_shift_store, k - LAG - 1)
+            run(scale_shift_store, k - LAG_STORE)
             run(regroup_ctx, k)
             run(first_product, k + 1)
-            run(inverse_deviation, k - LAG)
-            run(centre_and_gain, k - LAG)
+            run(inverse_deviation, k - LAG_DEVIATION)
+            run(centre_and_gain, k - LAG_ADD)
             run(quantise_ctx, k)
             for operand in operands:
                 quantise_operand(operand)

@@ -223,7 +223,7 @@ def tile_bertselfattention_pb_kernel(tc, probs, x, Wv, gamma, beta, out):
                 accum_out=y_sum[:],
             )
             minus_mean = work.tile([P, 1], F32, tag="minus_mean")
-            nc.vector.tensor_scalar_mul(minus_mean[:], y_sum[:], -1.0 / WIDTH)
+            nc.gpsimd.tensor_scalar_mul(minus_mean[:], y_sum[:], -1.0 / WIDTH)
             live["y", n] = y
             live["minus_mean", n] = minus_mean
 
@@ -239,7 +239,7 @@ def tile_bertselfattention_pb_kernel(tc, probs, x, Wv, gamma, beta, out):
             )
             live["centred", n] = centred
 
-        def inverse_deviation(n):
+        def sum_squares(n):
             squares = work.tile([P, WIDTH], BF16, tag="squares")
             square_sum = work.tile([P, 1], F32, tag="square_sum")
             nc.scalar.activation(
@@ -250,9 +250,14 @@ def tile_bertselfattention_pb_kernel(tc, probs, x, Wv, gamma, beta, out):
                 scale=1.0,
                 accum_out=square_sum[:],
             )
+            live["square_sum", n] = square_sum
+
+        def inverse_deviation(n):
             inv_std = work.tile([P, 1], F32, tag="inv_std")
             nc.scalar.activation(
-                out=inv_std[:], in_=square_sum[:], func=ACT.Abs_reciprocal_sqrt, bias=eps[:], scale=1.0 / WIDTH
+                out=inv_std[:],
+                in_=live["square_sum", n][:],
+                func=ACT.Abs_reciprocal_sqrt, bias=eps[:], scale=1.0 / WIDTH
             )
             live["inv_std", n] = inv_std
 
@@ -278,6 +283,7 @@ def tile_bertselfattention_pb_kernel(tc, probs, x, Wv, gamma, beta, out):
             operands = operands_of_round(k)
             run(second_product, k - LAG_ADD)
             run(regroup_probs, k + 1)
+            run(inverse_deviation, k - LAG_STORE)
             if k == FIRST_ROUND + 1:
                 spread_gain_and_shift()
             run(transpose_probs, k + 2)
@@ -288,7 +294,7 @@ def tile_bertselfattention_pb_kernel(tc, probs, x, Wv, gamma, beta, out):
             run(scale_shift_store, k - LAG_STORE)
             run(regroup_ctx, k)
             run(first_product, k + 1)
-            run(inverse_deviation, k - LAG_DEVIATION)
+            run(sum_squares, k - LAG_DEVIATION)
             run(centre_and_gain, k - LAG_ADD)
             run(quantise_ctx, k)
             for operand in operands:

@@ -27,10 +27,11 @@ D_PIECES = WIDTH // P
 HEADS_PER_BANK = 2
 RUN = 4
 LN_EPS = 1e-5
-FIRST_ROUND = -2
 LAG_ADD = 2
-LAG_DEVIATION = 3
+LAG_CENTRE = 3
 LAG_STORE = 4
+FIRST_ADD_ROUND = 3
+FIRST_SHARED = 4
 
 
 def tile_bertselfattention_pb_kernel(tc, probs, x, Wv, gamma, beta, out):
@@ -61,16 +62,6 @@ def tile_bertselfattention_pb_kernel(tc, probs, x, Wv, gamma, beta, out):
 
         x_operands = [leading_operand("x%d" % b, x_rows[b]) for b in range(BATCHES)]
         wv_operands = [leading_operand("wv%d" % h, wv_rows[h]) for h in range(HEADS)]
-        in_order_of_need = [x_operands[0]] + wv_operands + [x_operands[1]]
-
-        def operands_of_round(k):
-            if k == FIRST_ROUND:
-                return in_order_of_need[0:1]
-            if k == FIRST_ROUND + 1:
-                return in_order_of_need[1:3]
-            following = k - FIRST_ROUND + 1
-            return in_order_of_need[following : following + 1]
-
         def load_operand(operand):
             runs = operand["source"].shape[1]
             nc.sync.dma_start(
@@ -91,47 +82,63 @@ def tile_bertselfattention_pb_kernel(tc, probs, x, Wv, gamma, beta, out):
         def quantise_operand(operand):
             quantise(operand["grouped"], operand["codes"], operand["scales"])
 
+        identity = const.tile([P, P], F32)
+        make_identity(nc, identity[:])
         gain_shift_row = const.tile([P, 2 * WIDTH], BF16)
         nc.vector.memset(gain_shift_row[:], 0.0)
+        ones = const.tile([P, P], BF16)
+        nc.gpsimd.memset(ones[:], 1.0)
+        eps = const.tile([P, 1], F32)
+        nc.gpsimd.memset(eps[:], LN_EPS)
+
+        nc.scalar.dma_start(out=gain_shift_row[0:1, 0:WIDTH], in_=gamma.unsqueeze(0))
+        nc.scalar.dma_start(out=gain_shift_row[0:1, WIDTH : 2 * WIDTH], in_=beta.unsqueeze(0))
 
         probs_raw = [
             resident.tile([P, HEADS * TOKENS], BF16, name="probs_raw%d" % n) for n in range(UNITS)
         ]
-        for n in range(UNITS):
+
+        def load_probs(n, first_head, heads):
             b, place = divmod(n, UNITS_PER_BATCH)
             u, e = divmod(place, PAIR)
             nc.sync.dma_start(
-                out=probs_raw[n][:].rearrange("p (h j) -> p h j", h=HEADS), in_=probs_rows[b, u, e]
+                out=probs_raw[n][:].rearrange("p (h j) -> p h j", h=HEADS)[:, first_head : first_head + heads],
+                in_=probs_rows[b, u, e][:, first_head : first_head + heads],
             )
-            for operand in operands_of_round(n + FIRST_ROUND):
-                load_operand(operand)
-            if n == 0:
-                nc.sync.dma_start(out=gain_shift_row[0:1, 0:WIDTH], in_=gamma.unsqueeze(0))
-                nc.sync.dma_start(out=gain_shift_row[0:1, WIDTH : 2 * WIDTH], in_=beta.unsqueeze(0))
 
-        identity = const.tile([P, P], F32)
-        make_identity(nc, identity[:])
-        ones = const.tile([P, P], BF16)
-        nc.vector.memset(ones[:], 1.0)
-        eps = const.tile([P, 1], F32)
-        nc.vector.memset(eps[:], LN_EPS)
+        load_operand(x_operands[0])
+        for first_head in range(0, HEADS, HEADS_PER_BANK):
+            load_probs(0, first_head, HEADS_PER_BANK)
+        load_probs(1, 0, HEADS)
+        load_operand(wv_operands[0])
+        load_operand(wv_operands[1])
+        load_probs(2, 0, HEADS)
+        load_operand(wv_operands[2])
+        load_operand(wv_operands[3])
+        load_probs(3, 0, HEADS)
+        load_probs(4, 0, HEADS)
+        load_operand(x_operands[1])
+        for n in range(5, UNITS):
+            load_probs(n, 0, HEADS)
+
         table_warm = const.tile([P, 1], F32)
         nc.scalar.activation(out=table_warm[:], in_=eps[:], func=ACT.Abs_reciprocal_sqrt)
 
-        gain = const.tile([P, WIDTH], F32)
-        shift = const.tile([P, WIDTH], F32)
+        gain_shift = const.tile([P, 2 * WIDTH], BF16)
+        gain = gain_shift[:, 0:WIDTH]
+        shift = gain_shift[:, WIDTH : 2 * WIDTH]
 
         def spread_gain_and_shift():
-            for spread, first_column in ((gain, 0), (shift, WIDTH)):
-                spread_ps = psum_y.tile([P, WIDTH], F32, tag="y_ps")
+            spread_ps = psum_y.tile([P, 2 * WIDTH], BF16, tag="y_ps")
+            for first_column in (0, WIDTH):
                 nc.tensor.matmul(
-                    out=spread_ps[:],
+                    out=spread_ps[:, first_column : first_column + WIDTH],
                     lhsT=ones[:],
                     rhs=gain_shift_row[:, first_column : first_column + WIDTH],
                     start=True,
                     stop=True,
                 )
-                nc.scalar.copy(out=spread[:], in_=spread_ps[:])
+            nc.scalar.copy(out=gain_shift[:], in_=spread_ps[:])
 
         live = {}
 
@@ -184,13 +191,25 @@ def tile_bertselfattention_pb_kernel(tc, probs, x, Wv, gamma, beta, out):
             grouped = stage.tile([P, HEADS * P * PACK], BF16, tag="ctx_grouped", align_bytes=64)
             by_head = grouped[:].rearrange("p (h i t) -> p h i t", h=HEADS, t=PACK)
             for h in range(HEADS):
-                nc.scalar.copy(out=by_head[:, h], in_=live["ctx_ps%d" % h, n][:].rearrange("p t i -> p i t"))
+                in_places = live["ctx_ps%d" % h, n][:].rearrange("p t i -> p i t")
+                if n >= FIRST_SHARED and h == HEADS - 1:
+                    nc.vector.tensor_copy(out=by_head[:, h], in_=in_places)
+                else:
+                    nc.scalar.copy(out=by_head[:, h], in_=in_places)
             live["ctx_grouped", n] = grouped
 
         def quantise_ctx(n):
             codes = work.tile([P, HEADS * P], U32, tag="ctx_codes", align_bytes=64)
             scales = work.tile([P, HEADS * P], U8, tag="ctx_scales", align_bytes=64)
-            quantise(live["ctx_grouped", n], codes, scales)
+            parts = 2 if n == UNITS - 1 else 1
+            columns = HEADS * P // parts
+            for part in range(parts):
+                own = slice(part * columns, (part + 1) * columns)
+                nc.vector.quantize_mx(
+                    out=codes[:, own].bitcast(FP8X4),
+                    scales=scales[:, own],
+                    in_=live["ctx_grouped", n][:, part * columns * PACK : (part + 1) * columns * PACK],
+                )
             live["ctx_codes", n] = codes
             live["ctx_scales", n] = scales
 
@@ -233,7 +252,7 @@ def tile_bertselfattention_pb_kernel(tc, probs, x, Wv, gamma, beta, out):
                 out=centred[:],
                 in0=live["y", n][:],
                 scalar=live["minus_mean", n][:],
-                in1=gain[:],
+                in1=gain,
                 op0=ALU.add,
                 op1=ALU.mult,
             )
@@ -269,33 +288,54 @@ def tile_bertselfattention_pb_kernel(tc, probs, x, Wv, gamma, beta, out):
                 out=result[:],
                 in0=live["centred", n][:],
                 scalar=live["inv_std", n][:],
-                in1=shift[:],
+                in1=shift,
                 op0=ALU.mult,
                 op1=ALU.add,
             )
             nc.sync.dma_start(out=out_rows[b, u, e], in_=result[:])
 
-        def run(step, n):
-            if 0 <= n < UNITS:
-                step(n)
+        def run(step, *units):
+            for n in units:
+                if 0 <= n < UNITS:
+                    step(n)
 
-        for k in range(FIRST_ROUND, UNITS + LAG_STORE):
-            operands = operands_of_round(k)
-            run(second_product, k - LAG_ADD)
-            run(regroup_probs, k + 1)
-            run(inverse_deviation, k - LAG_STORE)
-            if k == FIRST_ROUND + 1:
-                spread_gain_and_shift()
-            run(transpose_probs, k + 2)
+        w = wv_operands
+        operand_steps = {
+            0: ([(regroup_operand, w[0])], [(quantise_operand, w[0]), (regroup_operand, w[1])], [(quantise_operand, w[1])]),
+            1: ([], [(regroup_operand, w[2])], [(regroup_operand, w[3]), (quantise_operand, w[2])]),
+            2: ([], [(quantise_operand, w[3])], [(regroup_operand, x_operands[1])]),
+            3: ([], [(quantise_operand, x_operands[1])], []),
+        }
+
+        run(transpose_probs, 0)
+        run(regroup_probs, 0)
+        regroup_operand(x_operands[0])
+        quantise_operand(x_operands[0])
+        spread_gain_and_shift()
+        run(transpose_probs, 1)
+        run(regroup_probs, 1)
+        run(quantise_probs, 0)
+        run(first_product, 0)
+        run(transpose_probs, 2)
+
+        for k in range(UNITS + LAG_STORE):
+            added = [n for n in range(UNITS) if max(n + LAG_ADD, FIRST_ADD_ROUND) == k]
+            before, between, behind = operand_steps.get(k, ([], [], []))
+            for step, operand in before:
+                step(operand)
             run(quantise_probs, k + 1)
-            run(add_residual, k - LAG_ADD)
-            for operand in operands:
-                regroup_operand(operand)
-            run(scale_shift_store, k - LAG_STORE)
+            for step, operand in between:
+                step(operand)
+            run(second_product, *added)
             run(regroup_ctx, k)
+            run(inverse_deviation, k - LAG_STORE)
+            run(regroup_probs, k + 2)
             run(first_product, k + 1)
-            run(sum_squares, k - LAG_DEVIATION)
-            run(centre_and_gain, k - LAG_ADD)
+            run(transpose_probs, k + 3)
+            run(add_residual, *added)
+            run(scale_shift_store, k - LAG_STORE)
             run(quantise_ctx, k)
-            for operand in operands:
-                quantise_operand(operand)
+            run(sum_squares, k - LAG_CENTRE)
+            run(centre_and_gain, k - LAG_CENTRE)
+            for step, operand in behind:
+                step(operand)

@@ -27,11 +27,12 @@ D_PIECES = WIDTH // P
 HEADS_PER_BANK = 2
 RUN = 4
 LN_EPS = 1e-5
-LAG_ADD = 2
-LAG_CENTRE = 3
+LAG_ADD = 1
+LAG_CENTRE = 2
+LAG_SQUARES = 3
 LAG_STORE = 4
-FIRST_ADD_ROUND = 3
-FIRST_SHARED = 4
+FIRST_ADD_ROUND = 2
+FIRST_SHARED = 5
 
 
 def tile_bertselfattention_pb_kernel(tc, probs, x, Wv, gamma, beta, out):
@@ -318,24 +319,24 @@ def tile_bertselfattention_pb_kernel(tc, probs, x, Wv, gamma, beta, out):
         run(first_product, 0)
         run(transpose_probs, 2)
 
+        def in_round(k, lag):
+            return [n for n in range(UNITS) if max(n + LAG_ADD, FIRST_ADD_ROUND) + lag - LAG_ADD == k]
+
         for k in range(UNITS + LAG_STORE):
-            added = [n for n in range(UNITS) if max(n + LAG_ADD, FIRST_ADD_ROUND) == k]
-            before, between, behind = operand_steps.get(k, ([], [], []))
-            for step, operand in before:
+            first, second, last = operand_steps.get(k, ([], [], []))
+            for step, operand in first + second:
                 step(operand)
-            run(quantise_probs, k + 1)
-            for step, operand in between:
-                step(operand)
-            run(second_product, *added)
+            run(second_product, *in_round(k, LAG_ADD))
+            run(inverse_deviation, *in_round(k, LAG_STORE))
             run(regroup_ctx, k)
-            run(inverse_deviation, k - LAG_STORE)
-            run(regroup_probs, k + 2)
+            run(scale_shift_store, *in_round(k, LAG_STORE))
+            run(sum_squares, *in_round(k, LAG_SQUARES))
+            run(quantise_probs, k + 1)
             run(first_product, k + 1)
+            run(regroup_probs, k + 2)
             run(transpose_probs, k + 3)
-            run(add_residual, *added)
-            run(scale_shift_store, k - LAG_STORE)
-            run(quantise_ctx, k)
-            run(sum_squares, k - LAG_CENTRE)
-            run(centre_and_gain, k - LAG_CENTRE)
-            for step, operand in behind:
+            for step, operand in last:
                 step(operand)
+            run(quantise_ctx, k)
+            run(add_residual, *in_round(k, LAG_ADD))
+            run(centre_and_gain, *in_round(k, LAG_CENTRE))

@@ -242,9 +242,12 @@ def tile_bertselfattention_pb_kernel(tc, probs, x, Wv, gamma, beta, out):
                 op1=ALU.add,
                 accum_out=y_sum[:],
             )
-            minus_mean = work.tile([P, 1], F32, tag="minus_mean")
-            nc.gpsimd.tensor_scalar_mul(minus_mean[:], y_sum[:], -1.0 / WIDTH)
             live["y", n] = y
+            live["y_sum", n] = y_sum
+
+        def negate_mean(n):
+            minus_mean = work.tile([P, 1], F32, tag="minus_mean")
+            nc.scalar.mul(minus_mean[:], live["y_sum", n][:], -1.0 / WIDTH)
             live["minus_mean", n] = minus_mean
 
         def centre_and_gain(n):
@@ -331,6 +334,7 @@ def tile_bertselfattention_pb_kernel(tc, probs, x, Wv, gamma, beta, out):
             run(regroup_ctx, k)
             run(scale_shift_store, *in_round(k, LAG_STORE))
             run(sum_squares, *in_round(k, LAG_SQUARES))
+            run(negate_mean, *in_round(k, LAG_CENTRE))
             run(quantise_probs, k + 1)
             run(first_product, k + 1)
             run(regroup_probs, k + 2)

@@ -32,7 +32,7 @@ LAG_CENTRE = 2
 LAG_SQUARES = 3
 LAG_STORE = 4
 FIRST_ADD_ROUND = 2
-FIRST_SHARED = 5
+SHARED_UNITS = (4, 5)
 
 
 def tile_bertselfattention_pb_kernel(tc, probs, x, Wv, gamma, beta, out):
@@ -83,6 +83,8 @@ def tile_bertselfattention_pb_kernel(tc, probs, x, Wv, gamma, beta, out):
         def quantise_operand(operand):
             quantise(operand["grouped"], operand["codes"], operand["scales"])
 
+        zeros = const.tile([P, WIDTH], BF16)
+        nc.gpsimd.memset(zeros[:], 0.0)
         identity = const.tile([P, P], F32)
         make_identity(nc, identity[:])
         gain_shift_row = const.tile([P, 2 * WIDTH], BF16)
@@ -141,6 +143,11 @@ def tile_bertselfattention_pb_kernel(tc, probs, x, Wv, gamma, beta, out):
                 )
             nc.scalar.copy(out=gain_shift[:], in_=spread_ps[:])
 
+        def keep_tensor_busy(passes):
+            unread_ps = psum_y.tile([P, WIDTH], F32, tag="y_ps")
+            for repeat in range(passes):
+                nc.tensor.matmul(out=unread_ps[:], lhsT=zeros[:, 0:P], rhs=zeros[:], start=True, stop=True)
+
         live = {}
 
         def transpose_probs(n):
@@ -193,7 +200,7 @@ def tile_bertselfattention_pb_kernel(tc, probs, x, Wv, gamma, beta, out):
             by_head = grouped[:].rearrange("p (h i t) -> p h i t", h=HEADS, t=PACK)
             for h in range(HEADS):
                 in_places = live["ctx_ps%d" % h, n][:].rearrange("p t i -> p i t")
-                if n >= FIRST_SHARED and h == HEADS - 1:
+                if n in SHARED_UNITS and h == HEADS - 1:
                     nc.vector.tensor_copy(out=by_head[:, h], in_=in_places)
                 else:
                     nc.scalar.copy(out=by_head[:, h], in_=in_places)
@@ -311,6 +318,7 @@ def tile_bertselfattention_pb_kernel(tc, probs, x, Wv, gamma, beta, out):
             3: ([], [(quantise_operand, x_operands[1])], []),
         }
 
+        keep_tensor_busy(5)
         run(transpose_probs, 0)
         run(regroup_probs, 0)
         regroup_operand(x_operands[0])
@@ -320,6 +328,7 @@ def tile_bertselfattention_pb_kernel(tc, probs, x, Wv, gamma, beta, out):
         run(regroup_probs, 1)
         run(quantise_probs, 0)
         run(first_product, 0)
+        keep_tensor_busy(2)
         run(transpose_probs, 2)
 
         def in_round(k, lag):
@@ -338,6 +347,8 @@ def tile_bertselfattention_pb_kernel(tc, probs, x, Wv, gamma, beta, out):
             run(quantise_probs, k + 1)
             run(first_product, k + 1)
             run(regroup_probs, k + 2)
+            if k == 0:
+                keep_tensor_busy(2)
             run(transpose_probs, k + 3)
             for step, operand in last:
                 step(operand)

@@ -32,6 +32,7 @@ LAG_CENTRE = 2
 LAG_SQUARES = 3
 LAG_STORE = 4
 FIRST_ADD_ROUND = 2
+TENSOR_UNIT = 4
 SHARED_UNITS = (4, 5)
 
 
@@ -110,15 +111,14 @@ def tile_bertselfattention_pb_kernel(tc, probs, x, Wv, gamma, beta, out):
             )
 
         load_operand(x_operands[0])
-        for first_head in range(0, HEADS, HEADS_PER_BANK):
-            load_probs(0, first_head, HEADS_PER_BANK)
+        load_probs(0, 0, HEADS_PER_BANK)
+        load_probs(0, HEADS_PER_BANK, HEADS_PER_BANK)
         load_probs(1, 0, HEADS)
         load_operand(wv_operands[0])
         load_operand(wv_operands[1])
-        load_probs(2, 0, HEADS)
-        load_operand(wv_operands[2])
-        load_operand(wv_operands[3])
-        load_probs(3, 0, HEADS)
+        for n in (2, 3):
+            load_probs(n, 0, HEADS)
+            load_operand(wv_operands[n])
         load_probs(4, 0, HEADS)
         load_operand(x_operands[1])
         for n in range(5, UNITS):
@@ -305,6 +305,32 @@ def tile_bertselfattention_pb_kernel(tc, probs, x, Wv, gamma, beta, out):
             )
             nc.sync.dma_start(out=out_rows[b, u, e], in_=result[:])
 
+        def diagonal(n):
+            diag = work.tile([P, P], F32, tag="diag")
+            nc.scalar.activation(out=diag[:], in_=identity[:], func=ACT.Copy, scale=live["inv_std", n][:])
+            live["diag", n] = diag
+
+        def scale_shift_by_tensor(n):
+            result_ps = psum_t.tile([P, WIDTH], F32, tag="flipped")
+            nc.tensor.matmul(
+                out=result_ps[:], lhsT=live["diag", n][:], rhs=live["centred", n][:], start=True, stop=False
+            )
+            nc.tensor.matmul(
+                out=result_ps[:],
+                lhsT=ones[:],
+                rhs=gain_shift_row[:, WIDTH : 2 * WIDTH],
+                start=False,
+                stop=True,
+            )
+            live["result_ps", n] = result_ps
+
+        def store_by_scalar(n):
+            b, place = divmod(n, UNITS_PER_BATCH)
+            u, e = divmod(place, PAIR)
+            result = work.tile([P, WIDTH], F32, tag="result")
+            nc.scalar.copy(out=result[:], in_=live["result_ps", n][:])
+            nc.scalar.dma_start(out=out_rows[b, u, e], in_=result[:])
+
         def run(step, *units):
             for n in units:
                 if 0 <= n < UNITS:
@@ -312,9 +338,13 @@ def tile_bertselfattention_pb_kernel(tc, probs, x, Wv, gamma, beta, out):
 
         w = wv_operands
         operand_steps = {
-            0: ([(regroup_operand, w[0])], [(quantise_operand, w[0]), (regroup_operand, w[1])], [(quantise_operand, w[1])]),
-            1: ([], [(regroup_operand, w[2])], [(regroup_operand, w[3]), (quantise_operand, w[2])]),
-            2: ([], [(quantise_operand, w[3])], [(regroup_operand, x_operands[1])]),
+            0: (
+                [(regroup_operand, w[0]), (regroup_operand, w[1])],
+                [(quantise_operand, w[0])],
+                [(quantise_operand, w[1])],
+            ),
+            1: ([], [(regroup_operand, w[2])], [(regroup_operand, w[3])]),
+            2: ([(quantise_operand, w[2]), (quantise_operand, w[3])], [], [(regroup_operand, x_operands[1])]),
             3: ([], [(quantise_operand, x_operands[1])], []),
         }
 
@@ -336,15 +366,23 @@ def tile_bertselfattention_pb_kernel(tc, probs, x, Wv, gamma, beta, out):
 
         for k in range(UNITS + LAG_STORE):
             first, second, last = operand_steps.get(k, ([], [], []))
-            for step, operand in first + second:
+            for step, operand in first:
                 step(operand)
             run(second_product, *in_round(k, LAG_ADD))
             run(inverse_deviation, *in_round(k, LAG_STORE))
+            if k == UNITS + LAG_STORE - 1:
+                store_by_scalar(TENSOR_UNIT)
             run(regroup_ctx, k)
-            run(scale_shift_store, *in_round(k, LAG_STORE))
+            ending = in_round(k, LAG_STORE)
+            by_tensor = [n for n in ending if n == TENSOR_UNIT]
             run(sum_squares, *in_round(k, LAG_SQUARES))
+            run(diagonal, *by_tensor)
             run(negate_mean, *in_round(k, LAG_CENTRE))
+            run(scale_shift_by_tensor, *by_tensor)
+            for step, operand in second:
+                step(operand)
             run(quantise_probs, k + 1)
+            run(scale_shift_store, *[n for n in ending if n != TENSOR_UNIT])
             run(first_product, k + 1)
             run(regroup_probs, k + 2)
             if k == 0:

from contextlib import ExitStack

import concourse.mybir as mybir
from concourse.masks import make_identity

FLOPS = 2 * 2 * 4 * 512 * 512 * 512 + 2 * 2 * 512 * 2048 * 512

F32 = mybir.dt.float32
BF16 = mybir.dt.bfloat16
U32 = mybir.dt.uint32
U8 = mybir.dt.uint8
FP8X4 = mybir.dt.float8_e4m3fn_x4
ALU = mybir.AluOpType
ACT = mybir.ActivationFunctionType

P = 128
PACK = 4
BATCHES = 2
HEADS = 4
TOKENS = 512
WIDTH = 512
HALVES = 2
PAIR = 2
UNITS_PER_BATCH = TOKENS // P
UNITS = BATCHES * UNITS_PER_BATCH
D_PIECES = WIDTH // P
HEADS_PER_BANK = 2
RUN = 4
LN_EPS = 1e-5
LAG_ADD = 1
LAG_CENTRE = 2
LAG_SQUARES = 3
LAG_STORE = 4
FIRST_ADD_ROUND = 2
TENSOR_UNIT = 4
SHARED_UNITS = (4, 5)


def tile_bertselfattention_pb_kernel(tc, probs, x, Wv, gamma, beta, out):
    nc = tc.nc

    probs_rows = probs.rearrange("b h (u p e) j -> b u e p h j", u=HALVES, e=PAIR)
    x_rows = x.rearrange("b (u p e) d -> b p u (e d)", u=HALVES, e=PAIR)
    out_rows = out.rearrange("b (u p e) d -> b u e p d", u=HALVES, e=PAIR)
    wv_rows = Wv.rearrange("(h t p) c -> h p t c", t=PACK, p=P)

    with ExitStack() as stack:
        const = stack.enter_context(tc.tile_pool(name="const", bufs=1))
        resident = stack.enter_context(tc.tile_pool(name="resident", bufs=1))
        stage = stack.enter_context(tc.tile_pool(name="stage", bufs=3))
        work = stack.enter_context(tc.tile_pool(name="work", bufs=LAG_STORE + 1))
        psum_t = stack.enter_context(tc.psum_pool(name="psum_t", bufs=HEADS // HEADS_PER_BANK))
        psum_ctx = stack.enter_context(tc.psum_pool(name="psum_ctx", bufs=HEADS))
        psum_y = stack.enter_context(tc.psum_pool(name="psum_y", bufs=2))
        stack.enter_context(tc.manual_schedule())

        def leading_operand(label, source):
            return {
                "source": source,
                "raw": resident.tile([P, PACK * WIDTH], BF16, name="raw_" + label),
                "codes": resident.tile([P, WIDTH], U32, name="codes_" + label, align_bytes=64),
                "scales": resident.tile([P, WIDTH], U8, name="scales_" + label, align_bytes=64),
            }

        x_operands = [leading_operand("x%d" % b, x_rows[b]) for b in range(BATCHES)]
        wv_operands = [leading_operand("wv%d" % h, wv_rows[h]) for h in range(HEADS)]
        def load_operand(operand):
            runs = operand["source"].shape[1]
            nc.sync.dma_start(
                out=operand["raw"][:].rearrange("p (r f) -> p r f", r=runs), in_=operand["source"]
            )

        def regroup_operand(operand):
            grouped = stage.tile([P, WIDTH * PACK], BF16, tag="operand_grouped", align_bytes=64)
            nc.vector.tensor_copy(
                out=grouped[:].rearrange("p (c i t) -> p c t i", i=RUN, t=PACK),
                in_=operand["raw"][:].rearrange("p (t c i) -> p c t i", t=PACK, i=RUN),
            )
            operand["grouped"] = grouped

        def quantise(grouped, codes, scales):
            nc.vector.quantize_mx(out=codes[:].bitcast(FP8X4), scales=scales[:], in_=grouped[:])

        def quantise_operand(operand):
            quantise(operand["grouped"], operand["codes"], operand["scales"])

        zeros = const.tile([P, WIDTH], BF16)
        nc.gpsimd.memset(zeros[:], 0.0)
        identity = const.tile([P, P], F32)
        make_identity(nc, identity[:])
        gain_shift_row = const.tile([P, 2 * WIDTH], BF16)
        nc.vector.memset(gain_shift_row[:], 0.0)
        ones = const.tile([P, P], BF16)
        nc.gpsimd.memset(ones[:], 1.0)
        eps = const.tile([P, 1], F32)
        nc.gpsimd.memset(eps[:], LN_EPS)

        nc.scalar.dma_start(out=gain_shift_row[0:1, 0:WIDTH], in_=gamma.unsqueeze(0))
        nc.scalar.dma_start(out=gain_shift_row[0:1, WIDTH : 2 * WIDTH], in_=beta.unsqueeze(0))

        probs_raw = [
            resident.tile([P, HEADS * TOKENS], BF16, name="probs_raw%d" % n) for n in range(UNITS)
        ]

        def load_probs(n, first_head, heads):
            b, place = divmod(n, UNITS_PER_BATCH)
            u, e = divmod(place, PAIR)
            nc.sync.dma_start(
                out=probs_raw[n][:].rearrange("p (h j) -> p h j", h=HEADS)[:, first_head : first_head + heads],
                in_=probs_rows[b, u, e][:, first_head : first_head + heads],
            )

        load_operand(x_operands[0])
        load_probs(0, 0, HEADS_PER_BANK)
        load_probs(0, HEADS_PER_BANK, HEADS_PER_BANK)
        load_probs(1, 0, HEADS)
        load_operand(wv_operands[0])
        load_operand(wv_operands[1])
        for n in (2, 3):
            load_probs(n, 0, HEADS)
            load_operand(wv_operands[n])
        load_probs(4, 0, HEADS)
        load_operand(x_operands[1])
        for n in range(5, UNITS):
            load_probs(n, 0, HEADS)

        table_warm = const.tile([P, 1], F32)
        nc.scalar.activation(out=table_warm[:], in_=eps[:], func=ACT.Abs_reciprocal_sqrt)

        gain_shift = const.tile([P, 2 * WIDTH], BF16)
        gain = gain_shift[:, 0:WIDTH]
        shift = gain_shift[:, WIDTH : 2 * WIDTH]

        def spread_gain_and_shift():
            spread_ps = psum_y.tile([P, 2 * WIDTH], BF16, tag="y_ps")
            for first_column in (0, WIDTH):
                nc.tensor.matmul(
                    out=spread_ps[:, first_column : first_column + WIDTH],
                    lhsT=ones[:],
                    rhs=gain_shift_row[:, first_column : first_column + WIDTH],
                    start=True,
                    stop=True,
                )
            nc.scalar.copy(out=gain_shift[:], in_=spread_ps[:])

        def keep_tensor_busy(passes):
            unread_ps = psum_y.tile([P, WIDTH], F32, tag="y_ps")
            for repeat in range(passes):
                nc.tensor.matmul(out=unread_ps[:], lhsT=zeros[:, 0:P], rhs=zeros[:], start=True, stop=True)

        live = {}

        def transpose_probs(n):
            words = probs_raw[n][:].bitcast(F32)
            for bank in range(HEADS // HEADS_PER_BANK):
                flipped = psum_t.tile([P, HEADS_PER_BANK, HALVES, P], F32, tag="flipped")
                for hh in range(HEADS_PER_BANK):
                    for u in range(HALVES):
                        first = ((bank * HEADS_PER_BANK + hh) * HALVES + u) * P
                        nc.tensor.transpose(flipped[:, hh, u, :], words[:, first : first + P], identity[:])
                live["flipped%d" % bank, n] = flipped

        def regroup_probs(n):
            grouped = stage.tile([P, HEADS * P * PACK], BF16, tag="probs_grouped", align_bytes=64)
            grouped_words = grouped[:].bitcast(F32).rearrange("p (h i u) -> p h i u", h=HEADS, u=HALVES)
            for bank in range(HEADS // HEADS_PER_BANK):
                nc.scalar.copy(
                    out=grouped_words[:, bank * HEADS_PER_BANK : (bank + 1) * HEADS_PER_BANK],
                    in_=live["flipped%d" % bank, n][:].rearrange("p h u i -> p h i u"),
                )
            live["probs_grouped", n] = grouped

        def quantise_probs(n):
            codes = stage.tile([P, HEADS * P], U32, tag="probs_codes", align_bytes=64)
            scales = stage.tile([P, HEADS * P], U8, tag="probs_scales", align_bytes=64)
            quantise(live["probs_grouped", n], codes, scales)
            live["probs_codes", n] = codes
            live["probs_scales", n] = scales

        def first_product(n):
            x_operand = x_operands[n // UNITS_PER_BATCH]
            for h in range(HEADS):
                tokens = slice(h * P, (h + 1) * P)
                ctx_ps = psum_ctx.tile([P, D_PIECES, P], F32, tag="ctx_ps")
                for t in range(D_PIECES):
                    d_columns = slice(t * P, (t + 1) * P)
                    nc.tensor.matmul_mx(
                        out=ctx_ps[:, t, :],
                        lhsT=x_operand["codes"][:, d_columns].bitcast(FP8X4),
                        lhsT_scale=x_operand["scales"][:, d_columns],
                        rhs=live["probs_codes", n][:, tokens].bitcast(FP8X4),
                        rhs_scale=live["probs_scales", n][:, tokens],
                        start=True,
                        stop=True,
                    )
                live["ctx_ps%d" % h, n] = ctx_ps

        def regroup_ctx(n):
            grouped = stage.tile([P, HEADS * P * PACK], BF16, tag="ctx_grouped", align_bytes=64)
            by_head = grouped[:].rearrange("p (h i t) -> p h i t", h=HEADS, t=PACK)
            for h in range(HEADS):
                in_places = live["ctx_ps%d" % h, n][:].rearrange("p t i -> p i t")
                if n in SHARED_UNITS and h == HEADS - 1:
                    nc.vector.tensor_copy(out=by_head[:, h], in_=in_places)
                else:
                    nc.scalar.copy(out=by_head[:, h], in_=in_places)
            live["ctx_grouped", n] = grouped

        def quantise_ctx(n):
            codes = work.tile([P, HEADS * P], U32, tag="ctx_codes", align_bytes=64)
            scales = work.tile([P, HEADS * P], U8, tag="ctx_scales", align_bytes=64)
            parts = 2 if n == UNITS - 1 else 1
            columns = HEADS * P // parts
            for part in range(parts):
                own = slice(part * columns, (part + 1) * columns)
                nc.vector.quantize_mx(
                    out=codes[:, own].bitcast(FP8X4),
                    scales=scales[:, own],
                    in_=live["ctx_grouped", n][:, part * columns * PACK : (part + 1) * columns * PACK],
                )
            live["ctx_codes", n] = codes
            live["ctx_scales", n] = scales

        def second_product(n):
            y_ps = psum_y.tile([P, WIDTH], F32, tag="y_ps")
            for h in range(HEADS):
                tokens = slice(h * P, (h + 1) * P)
                nc.tensor.matmul_mx(
                    out=y_ps[:],
                    lhsT=live["ctx_codes", n][:, tokens].bitcast(FP8X4),
                    lhsT_scale=live["ctx_scales", n][:, tokens],
                    rhs=wv_operands[h]["codes"][:].bitcast(FP8X4),
                    rhs_scale=wv_operands[h]["scales"][:],
                    start=(h == 0),
                    stop=(h == HEADS - 1),
                )
            live["y_ps", n] = y_ps

        def add_residual(n):
            b, place = divmod(n, UNITS_PER_BATCH)
            y = work.tile([P, WIDTH], F32, tag="y")
            y_sum = work.tile([P, 1], F32, tag="y_sum")
            nc.vector.scalar_tensor_tensor(
                out=y[:],
                in0=live["y_ps", n][:],
                scalar=1.0,
                in1=x_operands[b]["raw"][:, place * WIDTH : (place + 1) * WIDTH],
                op0=ALU.mult,
                op1=ALU.add,
                accum_out=y_sum[:],
            )
            live["y", n] = y
            live["y_sum", n] = y_sum

        def negate_mean(n):
            minus_mean = work.tile([P, 1], F32, tag="minus_mean")
            nc.scalar.mul(minus_mean[:], live["y_sum", n][:], -1.0 / WIDTH)
            live["minus_mean", n] = minus_mean

        def centre_and_gain(n):
            centred = work.tile([P, WIDTH], F32, tag="centred")
            nc.vector.scalar_tensor_tensor(
                out=centred[:],
                in0=live["y", n][:],
                scalar=live["minus_mean", n][:],
                in1=gain,
                op0=ALU.add,
                op1=ALU.mult,
            )
            live["centred", n] = centred

        def sum_squares(n):
            squares = work.tile([P, WIDTH], BF16, tag="squares")
            square_sum = work.tile([P, 1], F32, tag="square_sum")
            nc.scalar.activation(
                out=squares[:],
                in_=live["y", n][:],
                func=ACT.Square,
                bias=live["minus_mean", n][:],
                scale=1.0,
                accum_out=square_sum[:],
            )
            live["square_sum", n] = square_sum

        def inverse_deviation(n):
            inv_std = work.tile([P, 1], F32, tag="inv_std")
            nc.scalar.activation(
                out=inv_std[:],
                in_=live["square_sum", n][:],
                func=ACT.Abs_reciprocal_sqrt, bias=eps[:], scale=1.0 / WIDTH
            )
            live["inv_std", n] = inv_std

        def scale_shift_store(n):
            b, place = divmod(n, UNITS_PER_BATCH)
            u, e = divmod(place, PAIR)
            result = work.tile([P, WIDTH], F32, tag="result")
            nc.vector.scalar_tensor_tensor(
                out=result[:],
                in0=live["centred", n][:],
                scalar=live["inv_std", n][:],
                in1=shift,
                op0=ALU.mult,
                op1=ALU.add,
            )
            nc.sync.dma_start(out=out_rows[b, u, e], in_=result[:])

        def diagonal(n):
            diag = work.tile([P, P], F32, tag="diag")
            nc.scalar.activation(out=diag[:], in_=identity[:], func=ACT.Copy, scale=live["inv_std", n][:])
            live["diag", n] = diag

        def scale_shift_by_tensor(n):
            result_ps = psum_t.tile([P, WIDTH], F32, tag="flipped")
            nc.tensor.matmul(
                out=result_ps[:], lhsT=live["diag", n][:], rhs=live["centred", n][:], start=True, stop=False
            )
            nc.tensor.matmul(
                out=result_ps[:],
                lhsT=ones[:],
                rhs=gain_shift_row[:, WIDTH : 2 * WIDTH],
                start=False,
                stop=True,
            )
            live["result_ps", n] = result_ps

        def store_by_scalar(n):
            b, place = divmod(n, UNITS_PER_BATCH)
            u, e = divmod(place, PAIR)
            result = work.tile([P, WIDTH], F32, tag="result")
            nc.scalar.copy(out=result[:], in_=live["result_ps", n][:])
            nc.scalar.dma_start(out=out_rows[b, u, e], in_=result[:])

        def run(step, *units):
            for n in units:
                if 0 <= n < UNITS:
                    step(n)

        w = wv_operands
        operand_steps = {
            0: (
                [(regroup_operand, w[0]), (regroup_operand, w[1])],
                [(quantise_operand, w[0])],
                [(quantise_operand, w[1])],
            ),
            1: ([], [(regroup_operand, w[2])], [(regroup_operand, w[3])]),
            2: ([(quantise_operand, w[2]), (quantise_operand, w[3])], [], [(regroup_operand, x_operands[1])]),
            3: ([], [(quantise_operand, x_operands[1])], []),
        }

        keep_tensor_busy(5)
        run(transpose_probs, 0)
        run(regroup_probs, 0)
        regroup_operand(x_operands[0])
        quantise_operand(x_operands[0])
        spread_gain_and_shift()
        run(transpose_probs, 1)
        run(regroup_probs, 1)
        run(quantise_probs, 0)
        run(first_product, 0)
        keep_tensor_busy(2)
        run(transpose_probs, 2)

        def in_round(k, lag):
            return [n for n in range(UNITS) if max(n + LAG_ADD, FIRST_ADD_ROUND) + lag - LAG_ADD == k]

        for k in range(UNITS + LAG_STORE):
            first, second, last = operand_steps.get(k, ([], [], []))
            for step, operand in first:
                step(operand)
            run(second_product, *in_round(k, LAG_ADD))
            run(inverse_deviation, *in_round(k, LAG_STORE))
            if k == UNITS + LAG_STORE - 1:
                store_by_scalar(TENSOR_UNIT)
            run(regroup_ctx, k)
            ending = in_round(k, LAG_STORE)
            by_tensor = [n for n in ending if n == TENSOR_UNIT]
            run(sum_squares, *in_round(k, LAG_SQUARES))
            run(diagonal, *by_tensor)
            run(negate_mean, *in_round(k, LAG_CENTRE))
            run(scale_shift_by_tensor, *by_tensor)
            for step, operand in second:
                step(operand)
            run(quantise_probs, k + 1)
            run(scale_shift_store, *[n for n in ending if n != TENSOR_UNIT])
            run(first_product, k + 1)
            run(regroup_probs, k + 2)
            if k == 0:
                keep_tensor_busy(2)
            run(transpose_probs, k + 3)
            for step, operand in last:
                step(operand)
            run(quantise_ctx, k)
            run(add_residual, *in_round(k, LAG_ADD))
            run(centre_and_gain, *in_round(k, LAG_CENTRE))
